import numpy as np
import ml_dtypes


def mxq(x, axis, fmt="e4m3"):
    dtype, down = {"e4m3": (ml_dtypes.float8_e4m3fn, 7), "e5m2": (ml_dtypes.float8_e5m2, 14)}[fmt]
    v = np.moveaxis(np.asarray(x, np.float32).astype(ml_dtypes.bfloat16).astype(np.float64), axis, -1)
    blocks = v.reshape(v.shape[:-1] + (-1, 32))
    amax = np.abs(blocks).max(-1, keepdims=True)
    byte = np.maximum(np.where(amax > 0, np.frexp(amax)[1] - 1 + 127, 0) - down, 1)
    scale = np.exp2(byte - 127.0)
    codes = (blocks / scale).astype(np.float32).astype(dtype).astype(np.float64)
    return np.moveaxis((codes * scale).reshape(v.shape), -1, axis)


WIDE = False


def mx_kscale(k):
    if not WIDE:
        return np.ones(k)
    levels = np.array([18, -18])
    if k % 512:
        return np.exp2(np.random.permutation(np.resize(levels, k // 32))).repeat(32)
    a = np.empty((k // 512, 16))
    for p in range(k // 512):
        a[p, :8] = np.random.permutation(np.resize(levels, 8))
        for g in range(8):
            far = levels[np.abs(levels - a[p, g]) >= 10]
            a[p, g + 8] = far[np.random.randint(len(far))]
    return np.exp2(a.ravel()).repeat(32)


BF16 = ml_dtypes.bfloat16


def bf(x):
    return np.asarray(x, np.float32).astype(BF16)


def f64(x):
    return np.asarray(x).astype(np.float64)


B, T, H, DK, DH, E, V = 512, 1, 24, 64, 64, 1536, 1536
EPS = 1e-6


def setup_inputs():
    s = mx_kscale(B)[:, None]
    u = mx_kscale(E)
    w = np.repeat(mx_kscale(V), 2)[:V]
    x0 = bf(np.random.standard_normal((B, T, E)))
    qr = bf(np.random.standard_normal((B, H, T, DK)))
    kr = bf(np.random.standard_normal((B, H, T, DK)))
    decay = bf(np.random.uniform(0.7, 1.0, H))
    prev_kv = bf(np.random.standard_normal((1, H, DH, DK)))
    Wv0 = bf(np.random.standard_normal((E, V)) / np.sqrt(E))
    Wo0 = bf(np.random.standard_normal((V, E)) / np.sqrt(V))
    g = bf(np.random.standard_normal((B, E)) * np.exp2(np.random.randint(-6, 1, (B, 1))) / s * u)
    val = (f64(x0).reshape(B, E) @ f64(Wv0)).reshape(B, H, DH)
    q = f64(qr)[:, :, 0, :]
    k = f64(kr)[:, :, 0, :]
    old = np.einsum("bhc,hdc->bhd", q, f64(prev_kv)[0])
    r = f64(decay)[None, :, None] * old + np.sum(q * k, axis=2)[:, :, None] * val
    rstd = 1.0 / np.sqrt(np.mean(r * r, axis=2) + EPS)
    return {"x": bf(f64(x0) * s[:, :, None]),
            "qr": qr,
            "kr": kr,
            "decay": decay,
            "prev_kv": prev_kv,
            "Wv": bf(f64(Wv0) / w),
            "Wo": bf(f64(Wo0) * w[:, None] / u),
            "r": np.asarray(r, np.float32),
            "rstd": np.asarray(rstd, np.float32),
            "grad_out": g.reshape(B, T, E)}


def reference(x, qr, kr, decay, prev_kv, Wv, Wo, r, rstd, grad_out):
    g = f64(grad_out).reshape(B, E)
    dn = (mxq(g, 1, "e5m2") @ mxq(f64(Wo), 1, "e4m3").T).reshape(B, H, DH)
    rs = f64(rstd)[:, :, None]
    n = f64(r) * rs
    dr = rs * (dn - n * np.mean(dn * n, axis=2, keepdims=True))
    a = np.sum(f64(qr)[:, :, 0, :] * f64(kr)[:, :, 0, :], axis=2)[:, :, None]
    dv = (a * dr).reshape(B, V)
    dx = mxq(dv, 1, "e5m2") @ mxq(f64(Wv), 1, "e4m3").T
    dWv = mxq(f64(x).reshape(B, E), 0, "e4m3").T @ mxq(dv, 0, "e5m2")
    return dx.reshape(B, T, E), dWv

@@ -1,0 +1,592 @@
+from contextlib import ExitStack
+
+import concourse.mybir as mybir
+from concourse.masks import make_identity
+
+B, H, DH, E, V = 512, 24, 64, 1536, 1536
+FLOPS = 3 * 2 * B * E * V
+BYTES = 2 * (4 * B * E + 2 * E * V) + 4 * (B * V + B * H) + 4 * (B * E + E * V)
+
+F32 = mybir.dt.float32
+BF16 = mybir.dt.bfloat16
+U32 = mybir.dt.uint32
+U8 = mybir.dt.uint8
+E4M3 = mybir.dt.float8_e4m3fn_x4
+E5M2 = mybir.dt.float8_e5m2_x4
+ALU = mybir.AluOpType
+COPY = mybir.ActivationFunctionType.Copy
+AXIS_X = mybir.AxisListType.X
+
+P = 128
+PACK = 4
+N = P * PACK
+GROUPS = V // N
+HG = N // DH
+STEPS = GROUPS * PACK
+RAW_SLOTS = 8
+STAGE_SLOTS = 6
+OUT_SLOTS = 6
+BANKS = 6
+SCALAR_SUMS = 0
+
+
+def tile_multiscaleretention_pb_v_kernel(tc, x, qr, kr, decay, prev_kv, Wv, Wo, r, rstd, grad_out, out_0, out_1):
+    nc = tc.nc
+    with ExitStack() as ctx:
+        sb = ctx.enter_context(tc.tile_pool(name="sb", bufs=1))
+        ps = ctx.enter_context(tc.psum_pool(name="ps", bufs=1))
+        ctx.enter_context(tc.manual_schedule(engines={mybir.EngineType.SP}))
+
+        count = {}
+        tiles = {}
+        rings = {"dn": [0,1], "tr": [2,3,4,5,6,7], "mm": [0]}
+
+        def rotating(kind, slots, shape, dtype):
+            n = count.get(kind, 0)
+            count[kind] = n + 1
+            return sb.tile(shape, dtype, name="%s%d" % (kind, n), tag="%s%d" % (kind, n % slots), align_bytes=64)
+
+        def shared(kind, slots, shape, dtype):
+            n = count.get(kind, 0)
+            count[kind] = n + 1
+            return sb.tile(shape, dtype, name="%s%d" % (kind, n), tag=kind, bufs=slots, align_bytes=64)
+
+        def bank(kind, shape):
+            n = count.get(kind, 0)
+            count[kind] = n + 1
+            ring = rings[kind]
+            return ps.tile(shape, F32, name="%s%d" % (kind, n), tag="bank%d" % ring[n % len(ring)])
+
+        def fixed(name, shape, dtype):
+            return sb.tile(shape, dtype, name=name, tag=name, align_bytes=64)
+
+        def operand(name, width, fmt, tag=None):
+            codes = sb.tile([P, width], U32, name=name + "_codes", tag=(tag or name) + "_codes", align_bytes=64)
+            scales = sb.tile([P, width], U8, name=name + "_scales", tag=(tag or name) + "_scales", align_bytes=64)
+            return codes, scales, fmt
+
+        def copy(engine, out, in_):
+            if engine == "scalar":
+                nc.scalar.copy(out=out, in_=in_)
+            else:
+                nc.vector.tensor_copy(out=out, in_=in_)
+
+        def quantize(dst, window, src):
+            codes, scales, fmt = dst
+            nc.vector.quantize_mx(out=codes[:, window].bitcast(fmt), scales=scales[:, window], in_=src)
+
+        def mx_group(out, passes):
+            for n, (left, window, right) in enumerate(passes):
+                nc.tensor.matmul_mx(
+                    out=out,
+                    lhsT=left[0][:, window].bitcast(left[2]),
+                    lhsT_scale=left[1][:, window],
+                    rhs=right[0][:].bitcast(right[2]),
+                    rhs_scale=right[1][:],
+                    start=(n == 0),
+                    stop=(n == len(passes) - 1),
+                )
+
+        def cols(i, width):
+            return slice(i * width, (i + 1) * width)
+
+        by_token = "(p j) a b -> p j (a b)"
+        g_hbm = grad_out.rearrange(by_token, j=PACK)
+        x_hbm = x.rearrange(by_token, j=PACK)
+        r_hbm = r.rearrange(by_token, j=PACK)
+        q_hbm = qr.rearrange("(p j) h o c -> p j (h o c)", j=PACK)
+        k_hbm = kr.rearrange("(p j) h o c -> p j (h o c)", j=PACK)
+        dx_hbm = out_0.rearrange(by_token, j=PACK)
+        dw_hbm = out_1.rearrange("(m p) v -> p m v", p=P)
+
+        ident = fixed("ident", [P, P], F32)
+        make_identity(nc, ident[:])
+
+        g_mx = [operand("g%d" % c, N, E5M2) for c in range(GROUPS)]
+        wo_mx = [[operand("wo%d%d" % (g, c), N, E4M3) for c in range(GROUPS)] for g in range(GROUPS)]
+        wv_mx = {}
+        x_mx = operand("x", E, E4M3)
+        dvt_mx = [operand("dvt%d" % g, N, E5M2) for g in range(GROUPS)]
+        dv_mx = [operand("dv%d" % (g % 2), N, E5M2) for g in range(2)]
+        rs = fixed("rs", [P, PACK, H], F32)
+        neg_rs2 = fixed("neg_rs2", [P, PACK, H], F32)
+        x_raw = fixed("x_raw", [P, PACK, E], BF16)
+
+        def load(key, tile, src):
+            tiles[key] = tile
+            nc.sync.dma_start(out=tile[:], in_=src)
+
+        def load_g(half):
+            load(("g", half), rotating("raw", RAW_SLOTS, [P, 2, E], BF16), g_hbm[:, cols(half, 2), :])
+
+        def load_w(name, w, half):
+            src = w[cols(half, 2 * P), :].rearrange("(p i) k -> p i k", i=2)
+            load((name, half), rotating("raw", RAW_SLOTS, [P, 2, E], BF16), src)
+
+        def load_qk(g):
+            load(("q", g), rotating("q", 2, [P, PACK, N], BF16), q_hbm[:, :, cols(g, N)])
+            load(("k", g), rotating("k", 2, [P, PACK, N], BF16), k_hbm[:, :, cols(g, N)])
+
+        def load_r(g, halves=(0, 1)):
+            for half in halves:
+                load(("r", g, half), rotating("r", 4, [P, 2, N], F32), r_hbm[:, cols(half, 2), cols(g, N)])
+
+        def transpose_job(blocks, count_, order, dst, window):
+            held = {}
+
+            def tensor():
+                held["bank"] = bank("tr", [P, count_, 2, P])
+                for i, block in enumerate(blocks()):
+                    words = block.bitcast(F32)
+                    for u in range(2):
+                        nc.tensor.transpose(held["bank"][:, i, u, :], words[:, u::2], ident[:])
+
+            def evacuate(engine):
+                held["stage"] = rotating("stage", STAGE_SLOTS, [P, count_ * P * PACK], BF16)
+                src = held["bank"][:].rearrange(order)
+                dims = src.shape
+                words = held["stage"][:].bitcast(F32).rearrange("k (a b u) -> k a b u", a=dims[1], u=2)
+                copy(engine, words, src)
+
+            def follow():
+                quantize(dst(), window, held["stage"][:])
+
+            return tensor, evacuate, follow
+
+        def g_jobs(half):
+            return [
+                transpose_job(lambda c=c: [tiles["g", half][:, i, cols(c, N)] for i in range(2)], 2, "k i u p -> k i p u", lambda c=c: g_mx[c], cols(half, 2 * P))
+                for c in range(GROUPS)
+            ]
+
+        def w_jobs(name, dst, half):
+            return [
+                transpose_job(lambda c=c: [tiles[name, half][:, i, cols(c, N)] for i in range(2)], 2, "k i u p -> k p i u", lambda c=c: dst[half // 2][c], cols(half % 2, 2 * P))
+                for c in range(GROUPS)
+            ]
+
+        def dvt_job(g, first, n):
+            return transpose_job(lambda: [tiles["dv", g][:, cols(j, N)] for j in range(first, first + n)], n, "k i u p -> k i p u", lambda: dvt_mx[g], slice(first * P, (first + n) * P))
+
+        def output_job(key, slot, passes, dst, width=GROUPS):
+            held = {}
+
+            def tensor():
+                held["bank"] = bank("tr", [P, N])
+                mx_group(held["bank"][:], passes())
+
+            def evacuate(engine):
+                if slot == 0:
+                    tiles[key] = rotating("out", OUT_SLOTS, [P, width, N], F32)
+                copy(engine, tiles[key][:, slot, :], held["bank"][:])
+                if slot == width - 1:
+                    nc.sync.dma_start(out=dst, in_=tiles[key][:])
+
+            return tensor, evacuate, None
+
+        def dw_jobs(g):
+            return [
+                output_job(("dw", g, m // GROUPS), m % GROUPS, lambda m=m: [(x_mx, cols(m, P), dv_mx[g % 2])], dw_hbm[:, cols(m // GROUPS, GROUPS), cols(g, N)])
+                for m in range(E // P)
+            ]
+
+        def dx_jobs(j):
+            dst = dx_hbm[:, j, :].rearrange("p (e n) -> p e n", n=N)
+            return [output_job(("dx", j), e, lambda e=e: [(dvt_mx[g], cols(j, P), wv_mx[e][g]) for g in range(GROUPS)], dst) for e in range(GROUPS)]
+
+        def interleave(engine, src, kind, slots):
+            width = src.shape[2]
+            grouped = rotating(kind, slots, [P, width * PACK], BF16)
+            copy(
+                engine,
+                grouped[:].rearrange("p (c i t) -> p c t i", i=4, t=PACK),
+                src.rearrange("p t (c i) -> p c t i", i=4),
+            )
+            return grouped
+
+        def x_interleave(engine, n):
+            tiles["xg", n] = interleave(engine, x_raw[:, :, cols(n, 256)], "xg", 3)
+
+        def x_quantize(n):
+            quantize(x_mx, cols(n, 256), tiles["xg", n][:])
+
+        def dv_interleave(g):
+            tiles["dvg", g] = interleave("vector", tiles["dv", g][:].rearrange("p (j v) -> p j v", j=PACK), "dvg", 1)
+
+        def dv_quantize(g):
+            quantize(dv_mx[g % 2], slice(0, N), tiles["dvg", g][:])
+
+        def qk_product(g, half):
+            if half == 0:
+                tiles["qk", g] = rotating("qk", 1, [P, DH // 4, PACK * HG, 4], F32)
+            split = "p j (h hi lo) -> p (j h) hi lo"
+            nc.vector.tensor_tensor(
+                out=tiles["qk", g][:, :, cols(half, 2 * HG), :].rearrange("p hi a lo -> p a hi lo"),
+                in0=tiles["q", g][:, cols(half, 2), :].rearrange(split, h=HG, lo=4),
+                in1=tiles["k", g][:, cols(half, 2), :].rearrange(split, h=HG, lo=4),
+                op=ALU.mult,
+            )
+
+        def qk_jobs(g):
+            held = {}
+
+            def add_up():
+                held["sums"] = bank("tr", [P, P])
+                for hi in range(DH // 4):
+                    nc.tensor.matmul(
+                        out=held["sums"][:],
+                        lhsT=tiles["qk", g][:, hi].rearrange("p a lo -> p (a lo)"),
+                        rhs=ident[:],
+                        start=(hi == 0),
+                        stop=(hi == DH // 4 - 1),
+                        is_transpose=True,
+                    )
+
+            def keep(engine):
+                held["partial"] = rotating("partial", 1, [P, P], F32)
+                copy(engine, held["partial"][:], held["sums"][:])
+
+            def turn_back():
+                held["back"] = bank("tr", [P, P])
+                nc.tensor.transpose(held["back"][:], held["partial"][:], ident[:])
+
+            def finish(engine):
+                tiles["a", g] = fixed("a%d" % g, [P, PACK, HG], F32)
+                nc.vector.tensor_reduce(
+                    out=tiles["a", g][:].rearrange("p j h -> p (j h)"),
+                    in_=held["back"][:].rearrange("p (a lo) -> p a lo", lo=4),
+                    axis=AXIS_X,
+                    op=ALU.add,
+                )
+
+            return (add_up, keep, None), (turn_back, finish, lambda: gain(g))
+
+        def qk_sum_vector(g, half):
+            if half == 0:
+                tiles["a", g] = fixed("a%d" % g, [P, PACK, HG], F32)
+            nc.vector.tensor_reduce(
+                out=tiles["a", g][:, cols(half, 2), :].rearrange("p j h -> p (j h)"),
+                in_=tiles["qk", g][:, :, cols(half, 2 * HG), :].rearrange("p hi a lo -> p a hi lo"),
+                axis=mybir.AxisListType.XY,
+                op=ALU.add,
+            )
+
+        def gain(g):
+            tiles["gain", g] = fixed("gain%d" % g, [P, PACK, HG], F32)
+            nc.vector.tensor_tensor(out=tiles["gain", g][:], in0=tiles["a", g][:], in1=rs[:, :, cols(g, HG)], op=ALU.mult)
+
+        def dn_matmul(s):
+            g, j = divmod(s, PACK)
+            tiles["dn", s] = bank("dn", [P, N])
+            mx_group(tiles["dn", s][:], [(g_mx[c], cols(j, P), wo_mx[g][c]) for c in range(GROUPS)])
+
+        def dn_product(s):
+            g, j = divmod(s, PACK)
+            tiles["p", s] = rotating("w", 4, [P, N], F32)
+            nc.vector.tensor_tensor(out=tiles["p", s][:], in0=tiles["dn", s][:], in1=tiles["r", g, j // 2][:, j % 2, :], op=ALU.mult)
+
+        def dn_sum(s):
+            tiles["s", s] = rotating("s", 2, [P, HG], F32)
+            nc.vector.tensor_reduce(out=tiles["s", s][:], in_=tiles["p", s][:].rearrange("p (h d) -> p h d", d=DH), axis=AXIS_X, op=ALU.add)
+
+        def dn_mean(s):
+            g, j = divmod(s, PACK)
+            tiles["mu", s] = rotating("mu", 2, [P, HG], F32)
+            nc.vector.tensor_tensor(out=tiles["mu", s][:], in0=tiles["s", s][:], in1=neg_rs2[:, j, cols(g, HG)], op=ALU.mult)
+
+        def project(s):
+            g, j = divmod(s, PACK)
+            tiles["w", s] = tiles["p", s]
+            for h in range(HG):
+                nc.vector.scalar_tensor_tensor(
+                    out=tiles["w", s][:, cols(h, DH)],
+                    in0=tiles["r", g, j // 2][:, j % 2, cols(h, DH)],
+                    scalar=tiles["mu", s][:, h : h + 1],
+                    in1=tiles["dn", s][:, cols(h, DH)],
+                    op0=ALU.mult,
+                    op1=ALU.add,
+                )
+
+        def scale(s, engine="scalar"):
+            g, j = divmod(s, PACK)
+            if j == 0:
+                tiles["dv", g] = rotating("dv", 2, [P, PACK * N], BF16)
+            if engine == "vector":
+                nc.vector.tensor_tensor(
+                    out=tiles["dv", g][:, cols(j, N)].rearrange("p (h d) -> p h d", d=DH),
+                    in0=tiles["w", s][:].rearrange("p (h d) -> p h d", d=DH),
+                    in1=tiles["gain", g][:, j, :].unsqueeze(2).to_broadcast([P, HG, DH]),
+                    op=ALU.mult,
+                )
+                return
+            for h in range(HG):
+                nc.scalar.activation(
+                    out=tiles["dv", g][:, cols(j * HG + h, DH)],
+                    in_=tiles["w", s][:, cols(h, DH)],
+                    func=COPY,
+                    scale=tiles["gain", g][:, j, h : h + 1],
+                )
+
+        to_copy = []
+        to_follow = []
+
+        def pe(jobs):
+            for job in jobs:
+                job[0]()
+                to_copy.append(job)
+
+        def ev(n, engines="s"):
+            for i in range(min(n, len(to_copy))):
+                job = to_copy.pop(0)
+                job[1]("scalar" if engines[i % len(engines)] == "s" else "vector")
+                if job[2] is not None:
+                    to_follow.append(job[2])
+
+        def qz(n=99):
+            for i in range(min(n, len(to_follow))):
+                to_follow.pop(0)()
+
+        wo = [w_jobs("wo", wo_mx, half) for half in range(6)]
+        wv = [w_jobs("wv", wv_mx, half) for half in range(6)]
+        dw = [dw_jobs(g) for g in range(GROUPS)]
+        qk = [qk_jobs(g) for g in range(GROUPS)]
+
+        def qa(g):
+            qk[g][0][0]()
+
+        def qkeep(g):
+            qk[g][0][1]("scalar")
+
+        def qback(g):
+            qk[g][1][0]()
+
+        def qfin(g):
+            qk[g][1][1]("vector")
+
+        def wv_alloc(e):
+            wv_mx[e] = [operand("wv%d%d" % (e, g), N, E4M3, "wo%d%d" % (e, g) if e < 2 else None) for g in range(GROUPS)]
+
+        def dvt(g):
+            return [dvt_job(g, 0, 2), dvt_job(g, 2, 2)]
+
+        def load_x():
+            nc.sync.dma_start(out=x_raw[:], in_=x_hbm)
+
+        def load_wo(g):
+            load_w("wo", Wo, 2 * g)
+            load_w("wo", Wo, 2 * g + 1)
+
+        def load_wv(g):
+            load_w("wv", Wv, 2 * g)
+            load_w("wv", Wv, 2 * g + 1)
+
+        load_g(0)
+        load_wo(0)
+        nc.sync.dma_start(out=rs[:], in_=rstd.rearrange("(p j) h -> p j h", j=PACK))
+        load_r(0, (0,))
+        load_g(1)
+        load_qk(0)
+        load_r(0, (1,))
+        load_wo(1)
+        load_x()
+        load_qk(1)
+        load_r(1)
+        load_wo(2)
+        pe(g_jobs(0))
+        ev(3)
+        pe(wo[0])
+        ev(3)
+        qz(3)
+        nc.vector.scalar_tensor_tensor(out=neg_rs2[:].rearrange("p j h -> p (j h)"), in0=rs[:].rearrange("p j h -> p (j h)"), scalar=-1.0 / DH, in1=rs[:].rearrange("p j h -> p (j h)"), op0=ALU.mult, op1=ALU.mult)
+        pe(wo[1])
+        ev(3)
+        qz(3)
+        load_wv(0)
+        qz(3)
+        dn_matmul(0)
+        pe(g_jobs(1))
+        dn_matmul(1)
+        ev(3)
+        dn_product(0)
+        dn_sum(0)
+        qk_product(0,0)
+        dn_mean(0)
+        qk_product(0,1)
+        load_qk(2)
+        dn_product(1)
+        qz()
+        project(0)
+        qa(0)
+        qkeep(0)
+        dn_sum(1)
+        dn_mean(1)
+        dn_matmul(2)
+        pe(wo[2])
+        qback(0)
+        ev(3)
+        dn_product(2)
+        project(1)
+        qfin(0)
+        pe(wo[3])
+        load_wv(1)
+        ev(3)
+        dn_sum(2)
+        qz(3)
+        gain(0)
+        dn_mean(2)
+        dn_matmul(3)
+        scale(0)
+        scale(1)
+        dn_product(3)
+        qz(3)
+        project(2)
+        scale(2)
+        x_interleave("scalar", 0)
+        dn_sum(3)
+        dn_mean(3)
+        dn_matmul(4)
+        x_interleave("scalar", 1)
+        x_interleave("scalar", 2)
+        project(3)
+        x_quantize(0)
+        qk_product(1,0)
+        qk_product(1,1)
+        qa(1)
+        load_r(2)
+        scale(3)
+        qkeep(1)
+        x_interleave("scalar", 3)
+        dn_product(4)
+        x_quantize(1)
+        x_quantize(2)
+        dn_matmul(5)
+        pe(wo[4])
+        qback(1)
+        ev(3)
+        dn_sum(4)
+        dv_interleave(0)
+        dn_mean(4)
+        x_quantize(3)
+        qfin(1)
+        pe(dvt(0))
+        ev(2)
+        x_interleave("scalar", 4)
+        dn_product(5)
+        dv_quantize(0)
+        gain(1)
+        project(4)
+        qz(3)
+        pe(wo[5])
+        load_wv(2)
+        scale(4)
+        ev(3)
+        dn_sum(5)
+        qz(2)
+        dn_mean(5)
+        x_quantize(4)
+        dn_matmul(6)
+        pe(dw[0][0:3])
+        ev(3)
+        x_interleave("scalar", 5)
+        dn_product(6)
+        qz(3)
+        project(5)
+        wv_alloc(0)
+        pe(wv[0])
+        scale(5)
+        ev(3)
+        dn_sum(6)
+        x_quantize(5)
+        qk_product(2,0)
+        dn_mean(6)
+        dn_matmul(7)
+        pe(dw[0][3:6])
+        ev(3)
+        dn_product(7)
+        qz(3)
+        project(6)
+        qk_product(2,1)
+        pe(wv[1])
+        scale(6)
+        ev(3)
+        dn_sum(7)
+        qk_sum_vector(2,0)
+        dn_mean(7)
+        qk_sum_vector(2,1)
+        dn_matmul(8)
+        pe(dw[0][6:10])
+        ev(4)
+        dn_product(8)
+        qz(3)
+        project(7)
+        gain(2)
+        wv_alloc(1)
+        pe(wv[2])
+        scale(7)
+        ev(3)
+        dn_sum(8)
+        dn_mean(8)
+        dn_matmul(9)
+        pe(dw[0][10:12])
+        pe(dvt(1))
+        ev(4)
+        dv_interleave(1)
+        dn_product(9)
+        qz(3)
+        project(8)
+        dv_quantize(1)
+        pe(wv[3])
+        scale(8)
+        ev(3)
+        dn_sum(9)
+        qz(2)
+        dn_mean(9)
+        dn_matmul(10)
+        pe(dw[1][0:4])
+        ev(4,"sssv")
+        dn_product(10)
+        qz(3)
+        project(9)
+        wv_alloc(2)
+        pe(wv[4] + [dvt_job(2,0,1)])
+        ev(4)
+        dn_sum(10)
+        scale(9, "vector")
+        dn_mean(10)
+        dn_matmul(11)
+        pe(dw[1][4:8])
+        ev(4,"svsv")
+        dn_product(11)
+        qz(4)
+        project(10)
+        pe(wv[5] + [dvt_job(2,1,1)])
+        ev(4)
+        dn_sum(11)
+        scale(10, "vector")
+        dn_mean(11)
+        pe(dw[1][8:12])
+        ev(4)
+        qz(4)
+        project(11)
+        scale(11, "vector")
+        pe([dvt_job(2,2,1)])
+        pe(dx_jobs(0))
+        ev(4)
+        dv_interleave(2)
+        qz(1)
+        dv_quantize(2)
+        pe(dx_jobs(1))
+        pe([dvt_job(2,3,1)])
+        ev(4,"svss")
+        pe(dw[2][0:3])
+        pe(dx_jobs(2))
+        ev(6,"vs")
+        qz()
+        pe(dw[2][3:6])
+        ev(3,"vs")
+        pe(dx_jobs(3))
+        ev(3,"svs")
+        pe(dw[2][6:9])
+        ev(3,"vs")
+        pe(dw[2][9:12])
+        ev(3,"svs")

@@ -120,7 +120,7 @@ def tile_multiscaleretention_pb_v_kernel(tc, x, qr, kr, decay, prev_kv, Wv, Wo, 
             load(("g", half), rotating("raw", RAW_SLOTS, [P, 2, E], BF16), g_hbm[:, cols(half, 2), :])
 
         def load_w(name, w, half):
-            src = w[cols(half, 2 * P), :].rearrange("(p i) k -> p i k", i=2)
+            src = w[cols(half, 2 * P), :].rearrange("(i p) k -> p i k", i=2)
             load((name, half), rotating("raw", RAW_SLOTS, [P, 2, E], BF16), src)
 
         def load_qk(g):
@@ -131,7 +131,7 @@ def tile_multiscaleretention_pb_v_kernel(tc, x, qr, kr, decay, prev_kv, Wv, Wo, 
             for half in halves:
                 load(("r", g, half), rotating("r", 4, [P, 2, N], F32), r_hbm[:, cols(half, 2), cols(g, N)])
 
-        def transpose_job(blocks, count_, order, dst, window):
+        def transpose_job(blocks, count_, order, dst, window, sorted_words=False):
             held = {}
 
             def tensor():
@@ -139,7 +139,7 @@ def tile_multiscaleretention_pb_v_kernel(tc, x, qr, kr, decay, prev_kv, Wv, Wo, 
                 for i, block in enumerate(blocks()):
                     words = block.bitcast(F32)
                     for u in range(2):
-                        nc.tensor.transpose(held["bank"][:, i, u, :], words[:, u::2], ident[:])
+                        nc.tensor.transpose(held["bank"][:, i, u, :], words[:, cols(u, P)] if sorted_words else words[:, u::2], ident[:])
 
             def evacuate(engine):
                 held["stage"] = rotating("stage", STAGE_SLOTS, [P, count_ * P * PACK], BF16)
@@ -161,14 +161,14 @@ def tile_multiscaleretention_pb_v_kernel(tc, x, qr, kr, decay, prev_kv, Wv, Wo, 
 
         def w_jobs(name, dst, half):
             return [
-                transpose_job(lambda c=c: [tiles[name, half][:, i, cols(c, N)] for i in range(2)], 2, "k i u p -> k p i u", lambda c=c: dst[half // 2][c], cols(half % 2, 2 * P))
+                transpose_job(lambda c=c: [tiles[name, half][:, i, cols(c, N)] for i in range(2)], 2, "k i u p -> k i p u", lambda c=c: dst[half // 2][c], cols(half % 2, 2 * P))
                 for c in range(GROUPS)
             ]
 
         def dvt_job(g, first, n):
-            return transpose_job(lambda: [tiles["dv", g][:, cols(j, N)] for j in range(first, first + n)], n, "k i u p -> k i p u", lambda: dvt_mx[g], slice(first * P, (first + n) * P))
+            return transpose_job(lambda: [tiles["dv", g][:, cols(j, N)] for j in range(first, first + n)], n, "k i u p -> k i p u", lambda: dvt_mx[g], slice(first * P, (first + n) * P), True)
 
-        def output_job(key, slot, passes, dst, width=GROUPS):
+        def output_job(key, slot, passes, dst, sorted_columns=False, width=GROUPS):
             held = {}
 
             def tensor():
@@ -178,7 +178,10 @@ def tile_multiscaleretention_pb_v_kernel(tc, x, qr, kr, decay, prev_kv, Wv, Wo, 
             def evacuate(engine):
                 if slot == 0:
                     tiles[key] = rotating("out", OUT_SLOTS, [P, width, N], F32)
-                copy(engine, tiles[key][:, slot, :], held["bank"][:])
+                if sorted_columns:
+                    copy(engine, tiles[key][:, slot, :].rearrange("p (n u e) -> p n u e", u=2, e=2), held["bank"][:].rearrange("p (u n e) -> p n u e", u=2, e=2))
+                else:
+                    copy(engine, tiles[key][:, slot, :], held["bank"][:])
                 if slot == width - 1:
                     nc.sync.dma_start(out=dst, in_=tiles[key][:])
 
@@ -186,7 +189,7 @@ def tile_multiscaleretention_pb_v_kernel(tc, x, qr, kr, decay, prev_kv, Wv, Wo, 
 
         def dw_jobs(g):
             return [
-                output_job(("dw", g, m // GROUPS), m % GROUPS, lambda m=m: [(x_mx, cols(m, P), dv_mx[g % 2])], dw_hbm[:, cols(m // GROUPS, GROUPS), cols(g, N)])
+                output_job(("dw", g, m // GROUPS), m % GROUPS, lambda m=m: [(x_mx, cols(m, P), dv_mx[g % 2])], dw_hbm[:, cols(m // GROUPS, GROUPS), cols(g, N)], True)
                 for m in range(E // P)
             ]
 
@@ -312,17 +315,18 @@ def tile_multiscaleretention_pb_v_kernel(tc, x, qr, kr, decay, prev_kv, Wv, Wo, 
             if j == 0:
                 tiles["dv", g] = rotating("dv", 2, [P, PACK * N], BF16)
             if engine == "vector":
-                nc.vector.tensor_tensor(
-                    out=tiles["dv", g][:, cols(j, N)].rearrange("p (h d) -> p h d", d=DH),
-                    in0=tiles["w", s][:].rearrange("p (h d) -> p h d", d=DH),
-                    in1=tiles["gain", g][:, j, :].unsqueeze(2).to_broadcast([P, HG, DH]),
-                    op=ALU.mult,
-                )
+                for u in range(2):
+                    nc.vector.tensor_tensor(
+                        out=tiles["dv", g][:, cols(2 * j + u, N // 2)].rearrange("p (h n e) -> p h n e", h=HG, e=2),
+                        in0=tiles["w", s][:].rearrange("p (h n u e) -> p u h n e", h=HG, u=2, e=2)[:, u],
+                        in1=tiles["gain", g][:, j, :].unsqueeze(2).unsqueeze(3).to_broadcast([P, HG, DH // PACK, 2]),
+                        op=ALU.mult,
+                    )
                 return
             for h in range(HG):
                 nc.scalar.activation(
-                    out=tiles["dv", g][:, cols(j * HG + h, DH)],
-                    in_=tiles["w", s][:, cols(h, DH)],
+                    out=tiles["dv", g][:, cols(j, N)].rearrange("p (u n e) -> p u n e", u=2, e=2)[:, :, cols(h, DH // PACK), :],
+                    in_=tiles["w", s][:, cols(h, DH)].rearrange("p (n u e) -> p u n e", u=2, e=2),
                     func=COPY,
                     scale=tiles["gain", g][:, j, h : h + 1],
                 )
@@ -363,6 +367,27 @@ def tile_multiscaleretention_pb_v_kernel(tc, x, qr, kr, decay, prev_kv, Wv, Wo, 
         def qfin(g):
             qk[g][1][1]("vector")
 
+        def run(jobs, engines="s"):
+            for n, job in enumerate(jobs):
+                job[0]()
+                job[1]("scalar" if engines[n % len(engines)] == "s" else "vector")
+                if job[2] is not None:
+                    job[2]()
+
+        def chain(s):
+            dn_matmul(s)
+            dn_product(s)
+            dn_sum(s)
+            dn_mean(s)
+            project(s)
+
+        def a_vec(g):
+            qk_product(g, 0)
+            qk_product(g, 1)
+            qk_sum_vector(g, 0)
+            qk_sum_vector(g, 1)
+            gain(g)
+
         def wv_alloc(e):
             wv_mx[e] = [operand("wv%d%d" % (e, g), N, E4M3, "wo%d%d" % (e, g) if e < 2 else None) for g in range(GROUPS)]
 
@@ -380,213 +405,102 @@ def tile_multiscaleretention_pb_v_kernel(tc, x, qr, kr, decay, prev_kv, Wv, Wo, 
             load_w("wv", Wv, 2 * g)
             load_w("wv", Wv, 2 * g + 1)
 
+        load_qk(0)
         load_g(0)
         load_wo(0)
         nc.sync.dma_start(out=rs[:], in_=rstd.rearrange("(p j) h -> p j h", j=PACK))
         load_r(0, (0,))
         load_g(1)
-        load_qk(0)
         load_r(0, (1,))
         load_wo(1)
         load_x()
-        load_qk(1)
         load_r(1)
+        load_qk(1)
         load_wo(2)
-        pe(g_jobs(0))
-        ev(3)
-        pe(wo[0])
-        ev(3)
-        qz(3)
-        nc.vector.scalar_tensor_tensor(out=neg_rs2[:].rearrange("p j h -> p (j h)"), in0=rs[:].rearrange("p j h -> p (j h)"), scalar=-1.0 / DH, in1=rs[:].rearrange("p j h -> p (j h)"), op0=ALU.mult, op1=ALU.mult)
-        pe(wo[1])
-        ev(3)
-        qz(3)
-        load_wv(0)
-        qz(3)
-        dn_matmul(0)
-        pe(g_jobs(1))
-        dn_matmul(1)
-        ev(3)
-        dn_product(0)
-        dn_sum(0)
         qk_product(0,0)
-        dn_mean(0)
         qk_product(0,1)
-        load_qk(2)
-        dn_product(1)
-        qz()
-        project(0)
-        qa(0)
-        qkeep(0)
-        dn_sum(1)
-        dn_mean(1)
-        dn_matmul(2)
-        pe(wo[2])
-        qback(0)
-        ev(3)
-        dn_product(2)
-        project(1)
-        qfin(0)
-        pe(wo[3])
-        load_wv(1)
-        ev(3)
-        dn_sum(2)
-        qz(3)
+        run(g_jobs(0) + wo[0] + wo[1])
+        qk_sum_vector(0,0)
+        qk_sum_vector(0,1)
+        nc.vector.scalar_tensor_tensor(out=neg_rs2[:].rearrange("p j h -> p (j h)"), in0=rs[:].rearrange("p j h -> p (j h)"), scalar=-1.0 / DH, in1=rs[:].rearrange("p j h -> p (j h)"), op0=ALU.mult, op1=ALU.mult)
         gain(0)
-        dn_mean(2)
-        dn_matmul(3)
+        load_wv(0)
+        chain(0)
         scale(0)
+        chain(1)
         scale(1)
-        dn_product(3)
-        qz(3)
-        project(2)
+        run(g_jobs(1))
+        load_qk(2)
+        chain(2)
         scale(2)
-        x_interleave("scalar", 0)
-        dn_sum(3)
-        dn_mean(3)
-        dn_matmul(4)
-        x_interleave("scalar", 1)
-        x_interleave("scalar", 2)
-        project(3)
-        x_quantize(0)
-        qk_product(1,0)
-        qk_product(1,1)
-        qa(1)
-        load_r(2)
+        run(wo[2])
+        chain(3)
         scale(3)
-        qkeep(1)
-        x_interleave("scalar", 3)
-        dn_product(4)
-        x_quantize(1)
-        x_quantize(2)
-        dn_matmul(5)
-        pe(wo[4])
-        qback(1)
-        ev(3)
-        dn_sum(4)
+        run(wo[3])
+        load_wv(1)
+        load_r(2)
+        chain(4)
         dv_interleave(0)
-        dn_mean(4)
-        x_quantize(3)
-        qfin(1)
-        pe(dvt(0))
-        ev(2)
-        x_interleave("scalar", 4)
-        dn_product(5)
         dv_quantize(0)
-        gain(1)
-        project(4)
-        qz(3)
-        pe(wo[5])
-        load_wv(2)
+        x_interleave("scalar", 0)
+        x_quantize(0)
+        x_interleave("scalar", 1)
+        x_quantize(1)
+        run(dvt(0))
+        a_vec(1)
         scale(4)
-        ev(3)
-        dn_sum(5)
-        qz(2)
-        dn_mean(5)
-        x_quantize(4)
-        dn_matmul(6)
-        pe(dw[0][0:3])
-        ev(3)
-        x_interleave("scalar", 5)
-        dn_product(6)
-        qz(3)
-        project(5)
-        wv_alloc(0)
-        pe(wv[0])
+        load_wv(2)
+        chain(5)
         scale(5)
-        ev(3)
-        dn_sum(6)
-        x_quantize(5)
-        qk_product(2,0)
-        dn_mean(6)
-        dn_matmul(7)
-        pe(dw[0][3:6])
-        ev(3)
-        dn_product(7)
-        qz(3)
-        project(6)
-        qk_product(2,1)
-        pe(wv[1])
+        x_interleave("scalar", 2)
+        x_quantize(2)
+        x_interleave("scalar", 3)
+        x_quantize(3)
+        run(wo[4])
+        chain(6)
         scale(6)
-        ev(3)
-        dn_sum(7)
-        qk_sum_vector(2,0)
-        dn_mean(7)
-        qk_sum_vector(2,1)
-        dn_matmul(8)
-        pe(dw[0][6:10])
-        ev(4)
-        dn_product(8)
-        qz(3)
-        project(7)
-        gain(2)
-        wv_alloc(1)
-        pe(wv[2])
+        run(dw[0][0:4])
+        run(wo[5])
+        chain(7)
         scale(7)
-        ev(3)
-        dn_sum(8)
-        dn_mean(8)
-        dn_matmul(9)
-        pe(dw[0][10:12])
-        pe(dvt(1))
-        ev(4)
+        x_interleave("scalar", 4)
+        x_quantize(4)
+        x_interleave("scalar", 5)
+        x_quantize(5)
+        wv_alloc(0)
+        run(wv[0])
+        run(dw[0][4:8])
+        run(wv[1])
         dv_interleave(1)
-        dn_product(9)
-        qz(3)
-        project(8)
         dv_quantize(1)
-        pe(wv[3])
+        a_vec(2)
+        chain(8)
         scale(8)
-        ev(3)
-        dn_sum(9)
-        qz(2)
-        dn_mean(9)
-        dn_matmul(10)
-        pe(dw[1][0:4])
-        ev(4,"sssv")
-        dn_product(10)
-        qz(3)
-        project(9)
+        run(dw[0][8:12])
+        wv_alloc(1)
+        run(wv[2])
+        run(dw[1][0:3], "s")
+        run(wv[3])
+        chain(9)
+        scale(9)
+        run(dvt(1))
         wv_alloc(2)
-        pe(wv[4] + [dvt_job(2,0,1)])
-        ev(4)
-        dn_sum(10)
-        scale(9, "vector")
-        dn_mean(10)
-        dn_matmul(11)
-        pe(dw[1][4:8])
-        ev(4,"svsv")
-        dn_product(11)
-        qz(4)
-        project(10)
-        pe(wv[5] + [dvt_job(2,1,1)])
-        ev(4)
-        dn_sum(11)
-        scale(10, "vector")
-        dn_mean(11)
-        pe(dw[1][8:12])
-        ev(4)
-        qz(4)
-        project(11)
+        run(wv[4])
+        run(dw[1][3:6], "s")
+        run(wv[5])
+        chain(10)
+        scale(10)
+        run([dvt_job(2,0,2)])
+        run(dw[1][6:9], "s")
+        chain(11)
         scale(11, "vector")
-        pe([dvt_job(2,2,1)])
-        pe(dx_jobs(0))
-        ev(4)
         dv_interleave(2)
-        qz(1)
         dv_quantize(2)
-        pe(dx_jobs(1))
-        pe([dvt_job(2,3,1)])
-        ev(4,"svss")
-        pe(dw[2][0:3])
-        pe(dx_jobs(2))
-        ev(6,"vs")
-        qz()
-        pe(dw[2][3:6])
-        ev(3,"vs")
-        pe(dx_jobs(3))
-        ev(3,"svs")
-        pe(dw[2][6:9])
-        ev(3,"vs")
-        pe(dw[2][9:12])
-        ev(3,"svs")
+        run(dx_jobs(0), "s")
+        run(dw[1][9:12], "s")
+        run(dx_jobs(1), "s")
+        run([dvt_job(2,2,2)])
+        run(dw[2][0:6], "sv")
+        run(dx_jobs(2), "sv")
+        run(dw[2][6:12], "vs")
+        run(dx_jobs(3), "vs")

from contextlib import ExitStack

import concourse.mybir as mybir
from concourse.masks import make_identity

B, H, DH, E, V = 512, 24, 64, 1536, 1536
FLOPS = 3 * 2 * B * E * V
BYTES = 2 * (4 * B * E + 2 * E * V) + 4 * (B * V + B * H) + 4 * (B * E + E * V)

F32 = mybir.dt.float32
BF16 = mybir.dt.bfloat16
U32 = mybir.dt.uint32
U8 = mybir.dt.uint8
E4M3 = mybir.dt.float8_e4m3fn_x4
E5M2 = mybir.dt.float8_e5m2_x4
ALU = mybir.AluOpType
COPY = mybir.ActivationFunctionType.Copy
AXIS_X = mybir.AxisListType.X

P = 128
PACK = 4
N = P * PACK
GROUPS = V // N
HG = N // DH
STEPS = GROUPS * PACK
RAW_SLOTS = 8
STAGE_SLOTS = 6
OUT_SLOTS = 6
BANKS = 6
SCALAR_SUMS = 0


def tile_multiscaleretention_pb_v_kernel(tc, x, qr, kr, decay, prev_kv, Wv, Wo, r, rstd, grad_out, out_0, out_1):
    nc = tc.nc
    with ExitStack() as ctx:
        sb = ctx.enter_context(tc.tile_pool(name="sb", bufs=1))
        ps = ctx.enter_context(tc.psum_pool(name="ps", bufs=1))
        ctx.enter_context(tc.manual_schedule(engines={mybir.EngineType.SP}))

        count = {}
        tiles = {}
        rings = {"dn": [0,1], "tr": [2,3,4,5,6,7], "mm": [0]}

        def rotating(kind, slots, shape, dtype):
            n = count.get(kind, 0)
            count[kind] = n + 1
            return sb.tile(shape, dtype, name="%s%d" % (kind, n), tag="%s%d" % (kind, n % slots), align_bytes=64)

        def shared(kind, slots, shape, dtype):
            n = count.get(kind, 0)
            count[kind] = n + 1
            return sb.tile(shape, dtype, name="%s%d" % (kind, n), tag=kind, bufs=slots, align_bytes=64)

        def bank(kind, shape):
            n = count.get(kind, 0)
            count[kind] = n + 1
            ring = rings[kind]
            return ps.tile(shape, F32, name="%s%d" % (kind, n), tag="bank%d" % ring[n % len(ring)])

        def fixed(name, shape, dtype):
            return sb.tile(shape, dtype, name=name, tag=name, align_bytes=64)

        def operand(name, width, fmt, tag=None):
            codes = sb.tile([P, width], U32, name=name + "_codes", tag=(tag or name) + "_codes", align_bytes=64)
            scales = sb.tile([P, width], U8, name=name + "_scales", tag=(tag or name) + "_scales", align_bytes=64)
            return codes, scales, fmt

        def copy(engine, out, in_):
            if engine == "scalar":
                nc.scalar.copy(out=out, in_=in_)
            else:
                nc.vector.tensor_copy(out=out, in_=in_)

        def quantize(dst, window, src):
            codes, scales, fmt = dst
            nc.vector.quantize_mx(out=codes[:, window].bitcast(fmt), scales=scales[:, window], in_=src)

        def mx_group(out, passes):
            for n, (left, window, right) in enumerate(passes):
                nc.tensor.matmul_mx(
                    out=out,
                    lhsT=left[0][:, window].bitcast(left[2]),
                    lhsT_scale=left[1][:, window],
                    rhs=right[0][:].bitcast(right[2]),
                    rhs_scale=right[1][:],
                    start=(n == 0),
                    stop=(n == len(passes) - 1),
                )

        def cols(i, width):
            return slice(i * width, (i + 1) * width)

        by_token = "(p j) a b -> p j (a b)"
        g_hbm = grad_out.rearrange(by_token, j=PACK)
        x_hbm = x.rearrange(by_token, j=PACK)
        r_hbm = r.rearrange(by_token, j=PACK)
        q_hbm = qr.rearrange("(p j) h o c -> p j (h o c)", j=PACK)
        k_hbm = kr.rearrange("(p j) h o c -> p j (h o c)", j=PACK)
        dx_hbm = out_0.rearrange(by_token, j=PACK)
        dw_hbm = out_1.rearrange("(m p) v -> p m v", p=P)

        ident = fixed("ident", [P, P], F32)
        make_identity(nc, ident[:])

        g_mx = [operand("g%d" % c, N, E5M2) for c in range(GROUPS)]
        wo_mx = [[operand("wo%d%d" % (g, c), N, E4M3) for c in range(GROUPS)] for g in range(GROUPS)]
        wv_mx = {}
        x_mx = operand("x", E, E4M3)
        dvt_mx = [operand("dvt%d" % g, N, E5M2) for g in range(GROUPS)]
        dv_mx = [operand("dv%d" % (g % 2), N, E5M2) for g in range(2)]
        rs = fixed("rs", [P, PACK, H], F32)
        neg_rs2 = fixed("neg_rs2", [P, PACK, H], F32)
        x_raw = fixed("x_raw", [P, PACK, E], BF16)

        def load(key, tile, src):
            tiles[key] = tile
            nc.sync.dma_start(out=tile[:], in_=src)

        def load_g(half):
            load(("g", half), rotating("raw", RAW_SLOTS, [P, 2, E], BF16), g_hbm[:, cols(half, 2), :])

        def load_w(name, w, half):
            src = w[cols(half, 2 * P), :].rearrange("(i p) k -> p i k", i=2)
            load((name, half), rotating("raw", RAW_SLOTS, [P, 2, E], BF16), src)

        def load_qk(g):
            load(("q", g), rotating("q", 2, [P, PACK, N], BF16), q_hbm[:, :, cols(g, N)])
            load(("k", g), rotating("k", 2, [P, PACK, N], BF16), k_hbm[:, :, cols(g, N)])

        def load_r(g, halves=(0, 1)):
            for half in halves:
                load(("r", g, half), rotating("r", 4, [P, 2, N], F32), r_hbm[:, cols(half, 2), cols(g, N)])

        def transpose_job(blocks, count_, order, dst, window, sorted_words=False):
            held = {}

            def tensor():
                held["bank"] = bank("tr", [P, count_, 2, P])
                for i, block in enumerate(blocks()):
                    words = block.bitcast(F32)
                    for u in range(2):
                        nc.tensor.transpose(held["bank"][:, i, u, :], words[:, cols(u, P)] if sorted_words else words[:, u::2], ident[:])

            def evacuate(engine):
                held["stage"] = rotating("stage", STAGE_SLOTS, [P, count_ * P * PACK], BF16)
                src = held["bank"][:].rearrange(order)
                dims = src.shape
                words = held["stage"][:].bitcast(F32).rearrange("k (a b u) -> k a b u", a=dims[1], u=2)
                copy(engine, words, src)

            def follow():
                quantize(dst(), window, held["stage"][:])

            return tensor, evacuate, follow

        def g_jobs(half):
            return [
                transpose_job(lambda c=c: [tiles["g", half][:, i, cols(c, N)] for i in range(2)], 2, "k i u p -> k i p u", lambda c=c: g_mx[c], cols(half, 2 * P))
                for c in range(GROUPS)
            ]

        def w_jobs(name, dst, half):
            return [
                transpose_job(lambda c=c: [tiles[name, half][:, i, cols(c, N)] for i in range(2)], 2, "k i u p -> k i p u", lambda c=c: dst[half // 2][c], cols(half % 2, 2 * P))
                for c in range(GROUPS)
            ]

        def dvt_job(g, first, n):
            return transpose_job(lambda: [tiles["dv", g][:, cols(j, N)] for j in range(first, first + n)], n, "k i u p -> k i p u", lambda: dvt_mx[g], slice(first * P, (first + n) * P), True)

        def output_job(key, slot, passes, dst, sorted_columns=False, width=GROUPS):
            held = {}

            def tensor():
                held["bank"] = bank("tr", [P, N])
                mx_group(held["bank"][:], passes())

            def evacuate(engine):
                if slot == 0:
                    tiles[key] = rotating("out", OUT_SLOTS, [P, width, N], F32)
                if sorted_columns:
                    copy(engine, tiles[key][:, slot, :].rearrange("p (n u e) -> p n u e", u=2, e=2), held["bank"][:].rearrange("p (u n e) -> p n u e", u=2, e=2))
                else:
                    copy(engine, tiles[key][:, slot, :], held["bank"][:])
                if slot == width - 1:
                    nc.sync.dma_start(out=dst, in_=tiles[key][:])

            return tensor, evacuate, None

        def dw_jobs(g):
            return [
                output_job(("dw", g, m // GROUPS), m % GROUPS, lambda m=m: [(x_mx, cols(m, P), dv_mx[g % 2])], dw_hbm[:, cols(m // GROUPS, GROUPS), cols(g, N)], True)
                for m in range(E // P)
            ]

        def dx_jobs(j):
            dst = dx_hbm[:, j, :].rearrange("p (e n) -> p e n", n=N)
            return [output_job(("dx", j), e, lambda e=e: [(dvt_mx[g], cols(j, P), wv_mx[e][g]) for g in range(GROUPS)], dst) for e in range(GROUPS)]

        def interleave(engine, src, kind, slots):
            width = src.shape[2]
            grouped = rotating(kind, slots, [P, width * PACK], BF16)
            copy(
                engine,
                grouped[:].rearrange("p (c i t) -> p c t i", i=4, t=PACK),
                src.rearrange("p t (c i) -> p c t i", i=4),
            )
            return grouped

        def x_interleave(engine, n):
            tiles["xg", n] = interleave(engine, x_raw[:, :, cols(n, 256)], "xg", 3)

        def x_quantize(n):
            quantize(x_mx, cols(n, 256), tiles["xg", n][:])

        def dv_interleave(g):
            tiles["dvg", g] = interleave("vector", tiles["dv", g][:].rearrange("p (j v) -> p j v", j=PACK), "dvg", 1)

        def dv_quantize(g):
            quantize(dv_mx[g % 2], slice(0, N), tiles["dvg", g][:])

        def qk_product(g, half):
            if half == 0:
                tiles["qk", g] = rotating("qk", 1, [P, DH // 4, PACK * HG, 4], F32)
            split = "p j (h hi lo) -> p (j h) hi lo"
            nc.vector.tensor_tensor(
                out=tiles["qk", g][:, :, cols(half, 2 * HG), :].rearrange("p hi a lo -> p a hi lo"),
                in0=tiles["q", g][:, cols(half, 2), :].rearrange(split, h=HG, lo=4),
                in1=tiles["k", g][:, cols(half, 2), :].rearrange(split, h=HG, lo=4),
                op=ALU.mult,
            )

        def qk_jobs(g):
            held = {}

            def add_up():
                held["sums"] = bank("tr", [P, P])
                for hi in range(DH // 4):
                    nc.tensor.matmul(
                        out=held["sums"][:],
                        lhsT=tiles["qk", g][:, hi].rearrange("p a lo -> p (a lo)"),
                        rhs=ident[:],
                        start=(hi == 0),
                        stop=(hi == DH // 4 - 1),
                        is_transpose=True,
                    )

            def keep(engine):
                held["partial"] = rotating("partial", 1, [P, P], F32)
                copy(engine, held["partial"][:], held["sums"][:])

            def turn_back():
                held["back"] = bank("tr", [P, P])
                nc.tensor.transpose(held["back"][:], held["partial"][:], ident[:])

            def finish(engine):
                tiles["a", g] = fixed("a%d" % g, [P, PACK, HG], F32)
                nc.vector.tensor_reduce(
                    out=tiles["a", g][:].rearrange("p j h -> p (j h)"),
                    in_=held["back"][:].rearrange("p (a lo) -> p a lo", lo=4),
                    axis=AXIS_X,
                    op=ALU.add,
                )

            return (add_up, keep, None), (turn_back, finish, lambda: gain(g))

        def qk_sum_vector(g, half):
            if half == 0:
                tiles["a", g] = fixed("a%d" % g, [P, PACK, HG], F32)
            nc.vector.tensor_reduce(
                out=tiles["a", g][:, cols(half, 2), :].rearrange("p j h -> p (j h)"),
                in_=tiles["qk", g][:, :, cols(half, 2 * HG), :].rearrange("p hi a lo -> p a hi lo"),
                axis=mybir.AxisListType.XY,
                op=ALU.add,
            )

        def gain(g):
            tiles["gain", g] = fixed("gain%d" % g, [P, PACK, HG], F32)
            nc.vector.tensor_tensor(out=tiles["gain", g][:], in0=tiles["a", g][:], in1=rs[:, :, cols(g, HG)], op=ALU.mult)

        def dn_matmul(s):
            g, j = divmod(s, PACK)
            tiles["dn", s] = bank("dn", [P, N])
            mx_group(tiles["dn", s][:], [(g_mx[c], cols(j, P), wo_mx[g][c]) for c in range(GROUPS)])

        def dn_product(s):
            g, j = divmod(s, PACK)
            tiles["p", s] = rotating("w", 4, [P, N], F32)
            nc.vector.tensor_tensor(out=tiles["p", s][:], in0=tiles["dn", s][:], in1=tiles["r", g, j // 2][:, j % 2, :], op=ALU.mult)

        def dn_sum(s):
            tiles["s", s] = rotating("s", 2, [P, HG], F32)
            nc.vector.tensor_reduce(out=tiles["s", s][:], in_=tiles["p", s][:].rearrange("p (h d) -> p h d", d=DH), axis=AXIS_X, op=ALU.add)

        def dn_mean(s):
            g, j = divmod(s, PACK)
            tiles["mu", s] = rotating("mu", 2, [P, HG], F32)
            nc.vector.tensor_tensor(out=tiles["mu", s][:], in0=tiles["s", s][:], in1=neg_rs2[:, j, cols(g, HG)], op=ALU.mult)

        def project(s):
            g, j = divmod(s, PACK)
            tiles["w", s] = tiles["p", s]
            for h in range(HG):
                nc.vector.scalar_tensor_tensor(
                    out=tiles["w", s][:, cols(h, DH)],
                    in0=tiles["r", g, j // 2][:, j % 2, cols(h, DH)],
                    scalar=tiles["mu", s][:, h : h + 1],
                    in1=tiles["dn", s][:, cols(h, DH)],
                    op0=ALU.mult,
                    op1=ALU.add,
                )

        def scale(s, engine="scalar"):
            g, j = divmod(s, PACK)
            if j == 0:
                tiles["dv", g] = rotating("dv", 2, [P, PACK * N], BF16)
            if engine == "vector":
                for u in range(2):
                    nc.vector.tensor_tensor(
                        out=tiles["dv", g][:, cols(2 * j + u, N // 2)].rearrange("p (h n e) -> p h n e", h=HG, e=2),
                        in0=tiles["w", s][:].rearrange("p (h n u e) -> p u h n e", h=HG, u=2, e=2)[:, u],
                        in1=tiles["gain", g][:, j, :].unsqueeze(2).unsqueeze(3).to_broadcast([P, HG, DH // PACK, 2]),
                        op=ALU.mult,
                    )
                return
            for h in range(HG):
                nc.scalar.activation(
                    out=tiles["dv", g][:, cols(j, N)].rearrange("p (u n e) -> p u n e", u=2, e=2)[:, :, cols(h, DH // PACK), :],
                    in_=tiles["w", s][:, cols(h, DH)].rearrange("p (n u e) -> p u n e", u=2, e=2),
                    func=COPY,
                    scale=tiles["gain", g][:, j, h : h + 1],
                )

        to_copy = []
        to_follow = []

        def pe(jobs):
            for job in jobs:
                job[0]()
                to_copy.append(job)

        def ev(n, engines="s"):
            for i in range(min(n, len(to_copy))):
                job = to_copy.pop(0)
                job[1]("scalar" if engines[i % len(engines)] == "s" else "vector")
                if job[2] is not None:
                    to_follow.append(job[2])

        def qz(n=99):
            for i in range(min(n, len(to_follow))):
                to_follow.pop(0)()

        wo = [w_jobs("wo", wo_mx, half) for half in range(6)]
        wv = [w_jobs("wv", wv_mx, half) for half in range(6)]
        dw = [dw_jobs(g) for g in range(GROUPS)]
        qk = [qk_jobs(g) for g in range(GROUPS)]

        def qa(g):
            qk[g][0][0]()

        def qkeep(g):
            qk[g][0][1]("scalar")

        def qback(g):
            qk[g][1][0]()

        def qfin(g):
            qk[g][1][1]("vector")

        def run(jobs, engines="s"):
            for n, job in enumerate(jobs):
                job[0]()
                job[1]("scalar" if engines[n % len(engines)] == "s" else "vector")
                if job[2] is not None:
                    job[2]()

        def chain(s):
            dn_matmul(s)
            dn_product(s)
            dn_sum(s)
            dn_mean(s)
            project(s)

        def a_vec(g):
            qk_product(g, 0)
            qk_product(g, 1)
            qk_sum_vector(g, 0)
            qk_sum_vector(g, 1)
            gain(g)

        def wv_alloc(e):
            wv_mx[e] = [operand("wv%d%d" % (e, g), N, E4M3, "wo%d%d" % (e, g) if e < 2 else None) for g in range(GROUPS)]

        def dvt(g):
            return [dvt_job(g, 0, 2), dvt_job(g, 2, 2)]

        def load_x():
            nc.sync.dma_start(out=x_raw[:], in_=x_hbm)

        def load_wo(g):
            load_w("wo", Wo, 2 * g)
            load_w("wo", Wo, 2 * g + 1)

        def load_wv(g):
            load_w("wv", Wv, 2 * g)
            load_w("wv", Wv, 2 * g + 1)

        load_qk(0)
        load_g(0)
        load_wo(0)
        nc.sync.dma_start(out=rs[:], in_=rstd.rearrange("(p j) h -> p j h", j=PACK))
        load_r(0, (0,))
        load_g(1)
        load_r(0, (1,))
        load_wo(1)
        load_x()
        load_r(1)
        load_qk(1)
        load_wo(2)
        qk_product(0,0)
        qk_product(0,1)
        run(g_jobs(0) + wo[0] + wo[1])
        qk_sum_vector(0,0)
        qk_sum_vector(0,1)
        nc.vector.scalar_tensor_tensor(out=neg_rs2[:].rearrange("p j h -> p (j h)"), in0=rs[:].rearrange("p j h -> p (j h)"), scalar=-1.0 / DH, in1=rs[:].rearrange("p j h -> p (j h)"), op0=ALU.mult, op1=ALU.mult)
        gain(0)
        load_wv(0)
        chain(0)
        scale(0)
        chain(1)
        scale(1)
        run(g_jobs(1))
        load_qk(2)
        chain(2)
        scale(2)
        run(wo[2])
        chain(3)
        scale(3)
        run(wo[3])
        load_wv(1)
        load_r(2)
        chain(4)
        dv_interleave(0)
        dv_quantize(0)
        x_interleave("scalar", 0)
        x_quantize(0)
        x_interleave("scalar", 1)
        x_quantize(1)
        run(dvt(0))
        a_vec(1)
        scale(4)
        load_wv(2)
        chain(5)
        scale(5)
        x_interleave("scalar", 2)
        x_quantize(2)
        x_interleave("scalar", 3)
        x_quantize(3)
        run(wo[4])
        chain(6)
        scale(6)
        run(dw[0][0:4])
        run(wo[5])
        chain(7)
        scale(7)
        x_interleave("scalar", 4)
        x_quantize(4)
        x_interleave("scalar", 5)
        x_quantize(5)
        wv_alloc(0)
        run(wv[0])
        run(dw[0][4:8])
        run(wv[1])
        dv_interleave(1)
        dv_quantize(1)
        a_vec(2)
        chain(8)
        scale(8)
        run(dw[0][8:12])
        wv_alloc(1)
        run(wv[2])
        run(dw[1][0:3], "s")
        run(wv[3])
        chain(9)
        scale(9)
        run(dvt(1))
        wv_alloc(2)
        run(wv[4])
        run(dw[1][3:6], "s")
        run(wv[5])
        chain(10)
        scale(10)
        run([dvt_job(2,0,2)])
        run(dw[1][6:9], "s")
        chain(11)
        scale(11, "vector")
        dv_interleave(2)
        dv_quantize(2)
        run(dx_jobs(0), "s")
        run(dw[1][9:12], "s")
        run(dx_jobs(1), "s")
        run([dvt_job(2,2,2)])
        run(dw[2][0:6], "sv")
        run(dx_jobs(2), "sv")
        run(dw[2][6:12], "vs")
        run(dx_jobs(3), "vs")
